import numpy as np
import ml_dtypes

BF16 = ml_dtypes.bfloat16


def bf(x):
    return np.asarray(x, np.float32).astype(BF16)


def f32(x):
    return np.asarray(x, np.float32)


def f64(x):
    return np.asarray(x).astype(np.float64)


def striped(idx):
    return np.tile(idx.reshape(-1, 16).T, (8, 1))


D, S, B, N, H, P = 128, 4096, 512, 1024, 1024, 2
ERF_TERMS, ERF_CUT = 150, 6.0


def erf(a):
    c = np.clip(a, -ERF_CUT, ERF_CUT)
    term = c.copy()
    total = c.copy()
    for n in range(ERF_TERMS - 1):
        term = term * (2.0 * c * c) / (2 * n + 3)
        total = total + term
    val = 2.0 / np.sqrt(np.pi) * np.exp(-c * c) * total
    return np.where(np.abs(a) > ERF_CUT, np.sign(a), val)


def gelu(v):
    return 0.5 * v * (1.0 + erf(v / np.sqrt(2.0)))


def setup_inputs():
    return {
        "table": bf(np.random.standard_normal((D, S))),
        "w1": bf(np.random.standard_normal((D, D)) / np.sqrt(D)),
        "b1": f32(0.2 * np.random.standard_normal((D, 1))),
        "w2": bf(0.4 * np.random.standard_normal((D, D)) / np.sqrt(D)),
        "b2": f32(0.1 * np.random.standard_normal((D, 1))),
        "wb": bf(np.eye(D)[:, None, :] + 0.06 * np.random.standard_normal((D, D, D))),
        "ob": f32(0.3 * np.random.standard_normal((D, 1))),
        "wc1": bf(np.random.standard_normal((D, D)) / np.sqrt(D)),
        "bc1": f32(0.2 * np.random.standard_normal((D, 1))),
        "phenos": f32(np.random.standard_normal((P, B))),
        "wp1": f32(0.7 * np.random.standard_normal((H, P))),
        "wp2": bf(1.5 * np.random.standard_normal((H, H)) / np.sqrt(H)),
        "offs": striped(np.random.permutation(np.tile(np.arange(S), 2))[:N]),
    }


def reference(table, w1, b1, w2, b2, wb, ob, wc1, bc1, phenos, wp1, wp2, offs):
    idx = offs[:16].T.reshape(-1)
    a1 = np.maximum(f64(w1).T @ f64(table)[:, idx] + f64(b1), 0.0)
    h = f64(w2).T @ a1 + f64(b2)
    flat = f64(wb).reshape(D, D * D).T
    u = (flat @ h[:, :B]).reshape(D, D, B)
    v = (flat @ h[:, B:]).reshape(D, D, B)
    z = (u * v.transpose(1, 0, 2)).sum(axis=1) + f64(ob)
    top = np.maximum(f64(wc1).T @ z + f64(bc1), 0.0)
    q1 = gelu(f64(wp1) @ f64(phenos))
    q2 = gelu(f64(wp2).T @ q1)
    return np.concatenate([top, q2], axis=0)

@@ -1,0 +1,123 @@
+import concourse.mybir as mybir
+
+F32 = mybir.dt.float32
+BF16 = mybir.dt.bfloat16
+U16 = mybir.dt.uint16
+FN = mybir.ActivationFunctionType
+ALU = mybir.AluOpType
+
+D = 128
+S = 4096
+B = 512
+N = 2 * B
+H = 1024
+HC = H // D
+PIECE = B // 16
+
+FLOPS = 2 * (2 * D * D * N + 2 * D * D * D * B + D * D * B + 2 * H * B + H * H * B)
+
+
+def tile_bilinearmlpembedpheno_b_kernel(
+    tc, table, w1, b1, w2, b2, wb, ob, wc1, bc1, phenos, wp1, wp2, offs, out
+):
+    nc = tc.nc
+    with (
+        tc.tile_pool(name="held", bufs=1) as held,
+        tc.tile_pool(name="work", bufs=4) as work,
+        tc.psum_pool(name="psum_u", bufs=3) as psum_u,
+        tc.psum_pool(name="psum_v", bufs=3) as psum_v,
+        tc.psum_pool(name="psum_other", bufs=2) as psum_other,
+    ):
+        offsets = held.tile([D, N // 16], U16, name="offsets")
+        nc.sync.dma_start(offsets[:], offs)
+        w1_sb = held.tile([D, D], BF16, name="w1_sb")
+        nc.sync.dma_start(w1_sb[:], w1)
+        table_sb = held.tile([D, S], BF16, name="table_sb")
+        nc.sync.dma_start(table_sb[:], table)
+        w2_sb = held.tile([D, D], BF16, name="w2_sb")
+        nc.sync.dma_start(w2_sb[:], w2)
+        b1_sb = held.tile([D, 1], F32, name="b1_sb")
+        nc.sync.dma_start(b1_sb[:], b1)
+        b2_sb = held.tile([D, 1], F32, name="b2_sb")
+        nc.sync.dma_start(b2_sb[:], b2)
+        wp1_sb = held.tile([D, HC, 2], F32, name="wp1_sb")
+        nc.sync.dma_start(wp1_sb[:], wp1.rearrange("(p c) j -> p c j", c=HC))
+        ph_bc = held.tile([D, 2 * B], F32, name="ph_bc")
+        nc.sync.dma_start(ph_bc[:], phenos.rearrange("j t -> (j t)").partition_broadcast(D))
+        wb_sb = held.tile([D, D, D], BF16, name="wb_sb")
+        for q in range(4):
+            nc.sync.dma_start(wb_sb[:, q * 32 : (q + 1) * 32, :], wb[:, q * 32 : (q + 1) * 32, :])
+        wp2_sb = held.tile([D, HC, H], BF16, name="wp2_sb")
+        nc.sync.dma_start(wp2_sb[:], wp2.rearrange("(p c) y -> p c y", c=HC))
+        wc1_sb = held.tile([D, D], BF16, name="wc1_sb")
+        nc.sync.dma_start(wc1_sb[:], wc1)
+        ob_sb = held.tile([D, 1], F32, name="ob_sb")
+        nc.sync.dma_start(ob_sb[:], ob)
+        bc1_sb = held.tile([D, 1], F32, name="bc1_sb")
+        nc.sync.dma_start(bc1_sb[:], bc1)
+
+        ps_a1 = []
+        for half in range(2):
+            ps = psum_other.tile([D, B], F32, name=f"ps_a1_{half}", tag="other")
+            looked_up = table_sb[:].indirect(offsets[:, half * PIECE : (half + 1) * PIECE])
+            nc.tensor.matmul(ps[:], w1_sb[:], looked_up, start=True, stop=True)
+            ps_a1.append(ps)
+        h = []
+        for half in range(2):
+            a1 = work.tile([D, B], BF16, name="a1")
+            nc.scalar.activation(a1[:], ps_a1[half][:], FN.Relu, bias=b1_sb[:])
+            ps_h = psum_other.tile([D, B], F32, name="ps_h", tag="other")
+            nc.tensor.matmul(ps_h[:], w2_sb[:], a1[:], start=True, stop=True)
+            h_half = held.tile([D, B], BF16, name=f"h_{half}")
+            nc.vector.tensor_scalar_add(h_half[:], ps_h[:], b2_sb[:])
+            h.append(h_half)
+
+        q1 = held.tile([D, HC, B], BF16, name="q1")
+        for c in range(HC):
+            part = work.tile([D, B], F32, name="part")
+            nc.vector.tensor_scalar_mul(part[:], ph_bc[:, 0:B], wp1_sb[:, c, 0:1])
+            arg = work.tile([D, B], F32, name="arg")
+            nc.vector.scalar_tensor_tensor(
+                arg[:], ph_bc[:, B : 2 * B], wp1_sb[:, c, 1:2], part[:], op0=ALU.mult, op1=ALU.add
+            )
+            nc.scalar.activation(q1[:, c, :], arg[:], FN.Gelu)
+
+        def pheno_block(y):
+            ps_q2 = psum_other.tile([D, B], F32, name="ps_q2", tag="other")
+            for c in range(HC):
+                nc.tensor.matmul(
+                    ps_q2[:], wp2_sb[:, c, y * D : (y + 1) * D], q1[:, c, :],
+                    start=(c == 0), stop=(c == HC - 1),
+                )
+            q2 = work.tile([D, B], F32, name="q2")
+            nc.scalar.activation(q2[:], ps_q2[:], FN.Gelu)
+            nc.sync.dma_start(out[(y + 1) * D : (y + 2) * D, :], q2[:])
+
+        acc = [held.tile([D, B], F32, name=f"acc_{e}") for e in range(2)]
+        adders = [nc.vector, nc.gpsimd]
+        for a in range(D):
+            ps_u = psum_u.tile([D, B], F32, name="ps_u")
+            nc.tensor.matmul(ps_u[:], wb_sb[:, :, a], h[0][:], start=True, stop=True)
+            ps_v = psum_v.tile([D, B], F32, name="ps_v")
+            nc.tensor.matmul(ps_v[:], wb_sb[:, a, :], h[1][:], start=True, stop=True)
+            v_sb = work.tile([D, B], F32, name="v_sb")
+            nc.scalar.activation(v_sb[:], ps_v[:], FN.Copy)
+            e = a % 2
+            if a < 2:
+                nc.vector.tensor_tensor(acc[e][:], ps_u[:], v_sb[:], ALU.mult)
+            else:
+                prod = work.tile([D, B], F32, name="prod")
+                nc.vector.tensor_tensor(prod[:], ps_u[:], v_sb[:], ALU.mult)
+                adders[e].tensor_tensor(acc[e][:], acc[e][:], prod[:], ALU.add)
+            if a % (D // HC) == D // HC - 1:
+                pheno_block(a // (D // HC))
+
+        z = held.tile([D, B], BF16, name="z")
+        nc.vector.scalar_tensor_tensor(
+            z[:], acc[0][:], ob_sb[:], acc[1][:], op0=ALU.add, op1=ALU.add
+        )
+        ps_top = psum_other.tile([D, B], F32, name="ps_top", tag="other")
+        nc.tensor.matmul(ps_top[:], wc1_sb[:], z[:], start=True, stop=True)
+        top = work.tile([D, B], F32, name="top")
+        nc.scalar.activation(top[:], ps_top[:], FN.Relu, bias=bc1_sb[:])
+        nc.sync.dma_start(out[0:D, :], top[:])

@@ -1,4 +1,5 @@
 import concourse.mybir as mybir
+from concourse.masks import make_identity
 
 F32 = mybir.dt.float32
 BF16 = mybir.dt.bfloat16
@@ -13,6 +14,8 @@ N = 2 * B
 H = 1024
 HC = H // D
 PIECE = B // 16
+STRIDE = 16
+LAG = 4
 
 FLOPS = 2 * (2 * D * D * N + 2 * D * D * D * B + D * D * B + 2 * H * B + H * H * B)
 
@@ -24,9 +27,11 @@ def tile_bilinearmlpembedpheno_b_kernel(
     with (
         tc.tile_pool(name="held", bufs=1) as held,
         tc.tile_pool(name="work", bufs=4) as work,
+        tc.tile_pool(name="kept", bufs=2) as kept,
         tc.psum_pool(name="psum_u", bufs=3) as psum_u,
         tc.psum_pool(name="psum_v", bufs=3) as psum_v,
-        tc.psum_pool(name="psum_other", bufs=2) as psum_other,
+        tc.psum_pool(name="psum_other", bufs=1) as psum_other,
+        tc.psum_pool(name="psum_sum", bufs=1) as psum_sum,
     ):
         offsets = held.tile([D, N // 16], U16, name="offsets")
         nc.sync.dma_start(offsets[:], offs)
@@ -58,7 +63,7 @@ def tile_bilinearmlpembedpheno_b_kernel(
 
         ps_a1 = []
         for half in range(2):
-            ps = psum_other.tile([D, B], F32, name=f"ps_a1_{half}", tag="other")
+            ps = psum_u.tile([D, B], F32, name=f"ps_a1_{half}", tag="ps_u")
             looked_up = table_sb[:].indirect(offsets[:, half * PIECE : (half + 1) * PIECE])
             nc.tensor.matmul(ps[:], w1_sb[:], looked_up, start=True, stop=True)
             ps_a1.append(ps)
@@ -66,7 +71,7 @@ def tile_bilinearmlpembedpheno_b_kernel(
         for half in range(2):
             a1 = work.tile([D, B], BF16, name="a1")
             nc.scalar.activation(a1[:], ps_a1[half][:], FN.Relu, bias=b1_sb[:])
-            ps_h = psum_other.tile([D, B], F32, name="ps_h", tag="other")
+            ps_h = psum_v.tile([D, B], F32, name="ps_h", tag="ps_v")
             nc.tensor.matmul(ps_h[:], w2_sb[:], a1[:], start=True, stop=True)
             h_half = held.tile([D, B], BF16, name=f"h_{half}")
             nc.vector.tensor_scalar_add(h_half[:], ps_h[:], b2_sb[:])
@@ -93,6 +98,9 @@ def tile_bilinearmlpembedpheno_b_kernel(
             nc.scalar.activation(q2[:], ps_q2[:], FN.Gelu)
             nc.sync.dma_start(out[(y + 1) * D : (y + 2) * D, :], q2[:])
 
+        ident = held.tile([D, D], F32, name="ident")
+        make_identity(nc, ident[:])
+        ps_sum = psum_sum.tile([D, B], F32, name="ps_sum")
         acc = [held.tile([D, B], F32, name=f"acc_{e}") for e in range(2)]
         adders = [nc.vector, nc.gpsimd]
         for a in range(D):
@@ -105,17 +113,27 @@ def tile_bilinearmlpembedpheno_b_kernel(
             e = a % 2
             if a < 2:
                 nc.vector.tensor_tensor(acc[e][:], ps_u[:], v_sb[:], ALU.mult)
+            elif a % STRIDE == STRIDE // 2:
+                tensors = kept.tile([D, B], F32, name="tensors")
+                nc.vector.tensor_tensor(tensors[:], ps_u[:], v_sb[:], ALU.mult)
             else:
                 prod = work.tile([D, B], F32, name="prod")
                 nc.vector.tensor_tensor(prod[:], ps_u[:], v_sb[:], ALU.mult)
                 adders[e].tensor_tensor(acc[e][:], acc[e][:], prod[:], ALU.add)
+            if a % STRIDE == STRIDE // 2 + LAG:
+                nc.tensor.matmul(
+                    ps_sum[:], ident[:], tensors[:],
+                    start=(a < STRIDE), stop=(a > D - STRIDE),
+                )
             if a % (D // HC) == D // HC - 1:
                 pheno_block(a // (D // HC))
 
-        z = held.tile([D, B], BF16, name="z")
+        both = work.tile([D, B], F32, name="both")
         nc.vector.scalar_tensor_tensor(
-            z[:], acc[0][:], ob_sb[:], acc[1][:], op0=ALU.add, op1=ALU.add
+            both[:], ps_sum[:], ob_sb[:], acc[0][:], op0=ALU.add, op1=ALU.add
         )
+        z = held.tile([D, B], BF16, name="z")
+        nc.vector.tensor_tensor(z[:], both[:], acc[1][:], ALU.add)
         ps_top = psum_other.tile([D, B], F32, name="ps_top", tag="other")
         nc.tensor.matmul(ps_top[:], wc1_sb[:], z[:], start=True, stop=True)
         top = work.tile([D, B], F32, name="top")

@@ -6,6 +6,7 @@ BF16 = mybir.dt.bfloat16
 U16 = mybir.dt.uint16
 FN = mybir.ActivationFunctionType
 ALU = mybir.AluOpType
+AX = mybir.AxisListType
 
 D = 128
 S = 4096
@@ -14,8 +15,12 @@ N = 2 * B
 H = 1024
 HC = H // D
 PIECE = B // 16
-STRIDE = 16
-LAG = 4
+TB = B // D
+HALF = D // 2
+IG = HALF
+AG = B // IG
+IQ = B // D
+LEAD = 8
 
 FLOPS = 2 * (2 * D * D * N + 2 * D * D * D * B + D * D * B + 2 * H * B + H * H * B)
 
@@ -27,11 +32,11 @@ def tile_bilinearmlpembedpheno_b_kernel(
     with (
         tc.tile_pool(name="held", bufs=1) as held,
         tc.tile_pool(name="work", bufs=4) as work,
-        tc.tile_pool(name="kept", bufs=2) as kept,
+        tc.tile_pool(name="queue", bufs=10) as queue,
         tc.psum_pool(name="psum_u", bufs=3) as psum_u,
         tc.psum_pool(name="psum_v", bufs=3) as psum_v,
         tc.psum_pool(name="psum_other", bufs=1) as psum_other,
-        tc.psum_pool(name="psum_sum", bufs=1) as psum_sum,
+        tc.psum_pool(name="psum_z", bufs=1) as psum_z,
     ):
         offsets = held.tile([D, N // 16], U16, name="offsets")
         nc.sync.dma_start(offsets[:], offs)
@@ -49,9 +54,11 @@ def tile_bilinearmlpembedpheno_b_kernel(
         nc.sync.dma_start(wp1_sb[:], wp1.rearrange("(p c) j -> p c j", c=HC))
         ph_bc = held.tile([D, 2 * B], F32, name="ph_bc")
         nc.sync.dma_start(ph_bc[:], phenos.rearrange("j t -> (j t)").partition_broadcast(D))
-        wb_sb = held.tile([D, D, D], BF16, name="wb_sb")
-        for q in range(4):
-            nc.sync.dma_start(wb_sb[:, q * 32 : (q + 1) * 32, :], wb[:, q * 32 : (q + 1) * 32, :])
+        wb_half = []
+        for s in range(2):
+            wb_s = held.tile([D, HALF, D], BF16, name=f"wb_{s}")
+            nc.sync.dma_start(wb_s[:], wb[:, s * HALF : (s + 1) * HALF, :])
+            wb_half.append(wb_s)
         wp2_sb = held.tile([D, HC, H], BF16, name="wp2_sb")
         nc.sync.dma_start(wp2_sb[:], wp2.rearrange("(p c) y -> p c y", c=HC))
         wc1_sb = held.tile([D, D], BF16, name="wc1_sb")
@@ -60,6 +67,8 @@ def tile_bilinearmlpembedpheno_b_kernel(
         nc.sync.dma_start(ob_sb[:], ob)
         bc1_sb = held.tile([D, 1], F32, name="bc1_sb")
         nc.sync.dma_start(bc1_sb[:], bc1)
+        ident = held.tile([D, D], F32, name="ident")
+        make_identity(nc, ident[:])
 
         ps_a1 = []
         for half in range(2):
@@ -80,7 +89,7 @@ def tile_bilinearmlpembedpheno_b_kernel(
         q1 = held.tile([D, HC, B], BF16, name="q1")
         for c in range(HC):
             part = work.tile([D, B], F32, name="part")
-            nc.vector.tensor_scalar_mul(part[:], ph_bc[:, 0:B], wp1_sb[:, c, 0:1])
+            nc.scalar.activation(part[:], ph_bc[:, 0:B], FN.Copy, scale=wp1_sb[:, c, 0:1])
             arg = work.tile([D, B], F32, name="arg")
             nc.vector.scalar_tensor_tensor(
                 arg[:], ph_bc[:, B : 2 * B], wp1_sb[:, c, 1:2], part[:], op0=ALU.mult, op1=ALU.add
@@ -98,42 +107,66 @@ def tile_bilinearmlpembedpheno_b_kernel(
             nc.scalar.activation(q2[:], ps_q2[:], FN.Gelu)
             nc.sync.dma_start(out[(y + 1) * D : (y + 2) * D, :], q2[:])
 
-        ident = held.tile([D, D], F32, name="ident")
-        make_identity(nc, ident[:])
-        ps_sum = psum_sum.tile([D, B], F32, name="ps_sum")
-        acc = [held.tile([D, B], F32, name=f"acc_{e}") for e in range(2)]
-        adders = [nc.vector, nc.gpsimd]
-        for a in range(D):
-            ps_u = psum_u.tile([D, B], F32, name="ps_u")
-            nc.tensor.matmul(ps_u[:], wb_sb[:, :, a], h[0][:], start=True, stop=True)
-            ps_v = psum_v.tile([D, B], F32, name="ps_v")
-            nc.tensor.matmul(ps_v[:], wb_sb[:, a, :], h[1][:], start=True, stop=True)
-            v_sb = work.tile([D, B], F32, name="v_sb")
-            nc.scalar.activation(v_sb[:], ps_v[:], FN.Copy)
-            e = a % 2
-            if a < 2:
-                nc.vector.tensor_tensor(acc[e][:], ps_u[:], v_sb[:], ALU.mult)
-            elif a % STRIDE == STRIDE // 2:
-                tensors = kept.tile([D, B], F32, name="tensors")
-                nc.vector.tensor_tensor(tensors[:], ps_u[:], v_sb[:], ALU.mult)
-            else:
-                prod = work.tile([D, B], F32, name="prod")
-                nc.vector.tensor_tensor(prod[:], ps_u[:], v_sb[:], ALU.mult)
-                adders[e].tensor_tensor(acc[e][:], acc[e][:], prod[:], ALU.add)
-            if a % STRIDE == STRIDE // 2 + LAG:
-                nc.tensor.matmul(
-                    ps_sum[:], ident[:], tensors[:],
-                    start=(a < STRIDE), stop=(a > D - STRIDE),
-                )
-            if a % (D // HC) == D // HC - 1:
-                pheno_block(a // (D // HC))
+        zt = [held.tile([D, D], F32, name=f"zt_{tb}") for tb in range(TB)]
+        acc = [held.tile([D, IG, AG], F32, name=f"acc_{tb}") for tb in range(TB)]
 
-        both = work.tile([D, B], F32, name="both")
-        nc.vector.scalar_tensor_tensor(
-            both[:], ps_sum[:], ob_sb[:], acc[0][:], op0=ALU.add, op1=ALU.add
-        )
+        def unit_gpsimd(g, tb):
+            h_u = h[0][:, tb * D : (tb + 1) * D]
+            h_v = h[1][:, tb * D : (tb + 1) * D]
+            s, a0 = divmod(g * AG, HALF)
+            ps_v = psum_v.tile([D, AG, IG], F32, name="ps_v", tag="ps_v")
+            nc.tensor.matmul(ps_v[:], h_v, wb_half[s][:, a0 : a0 + AG, 0:IG], start=True, stop=True)
+            ps_u = psum_u.tile([D, IG, AG], F32, name="ps_u", tag="ps_u")
+            nc.tensor.matmul(
+                ps_u[:], h_u, wb_half[0][:, 0:IG, g * AG : (g + 1) * AG], start=True, stop=True
+            )
+            v_sb = work.tile([D, IG, AG], F32, name="v_sb")
+            nc.scalar.activation(v_sb[:], ps_v[:].rearrange("p a i -> p i a"), FN.Copy)
+            if g == 0:
+                nc.vector.tensor_tensor(acc[tb][:], ps_u[:], v_sb[:], ALU.mult)
+            else:
+                prod = queue.tile([D, IG, AG], F32, name="prod")
+                nc.vector.tensor_tensor(prod[:], ps_u[:], v_sb[:], ALU.mult)
+                nc.gpsimd.tensor_tensor(acc[tb][:], acc[tb][:], prod[:], ALU.add)
+
+        def unit_vector(q, tb):
+            h_u = h[0][:, tb * D : (tb + 1) * D]
+            h_v = h[1][:, tb * D : (tb + 1) * D]
+            i0 = IG + q * IQ
+            ps_v = psum_v.tile([D, D, IQ], F32, name="ps_v2", tag="ps_v")
+            for s in range(2):
+                nc.tensor.matmul(
+                    ps_v[:, s * HALF : (s + 1) * HALF, :], h_v, wb_half[s][:, :, i0 : i0 + IQ],
+                    start=True, stop=True,
+                )
+            ps_u = psum_u.tile([D, IQ, D], F32, name="ps_u2", tag="ps_u")
+            nc.tensor.matmul(
+                ps_u[:], h_u, wb_half[1][:, i0 - HALF : i0 - HALF + IQ, :], start=True, stop=True
+            )
+            v_sb = work.tile([D, IQ, D], F32, name="v_sb2", tag="v_sb")
+            nc.scalar.activation(v_sb[:], ps_v[:].rearrange("p a i -> p i a"), FN.Copy)
+            for r in range(IQ):
+                prod = work.tile([D, D], F32, name="prod_one")
+                nc.vector.scalar_tensor_tensor(
+                    prod[:], ps_u[:, r, :], 1.0, v_sb[:, r, :], op0=ALU.mult, op1=ALU.mult,
+                    accum_out=zt[tb][:, i0 + r : i0 + r + 1],
+                )
+
+        units = HALF
+        for step in range(units + LEAD):
+            if step < units:
+                unit_gpsimd(*divmod(step, TB))
+            if step >= LEAD:
+                unit_vector(*divmod(step - LEAD, TB))
+            if step >= LEAD and step % HC == HC - 1:
+                pheno_block(step // HC - 1)
+
+        ps_z = psum_z.tile([D, B], F32, name="ps_z")
+        for tb in range(TB):
+            nc.vector.tensor_reduce(zt[tb][:, 0:IG], acc[tb][:], axis=AX.X, op=ALU.add)
+            nc.tensor.transpose(ps_z[:, tb * D : (tb + 1) * D], zt[tb][:], ident[:])
         z = held.tile([D, B], BF16, name="z")
-        nc.vector.tensor_tensor(z[:], both[:], acc[1][:], ALU.add)
+        nc.scalar.activation(z[:], ps_z[:], FN.Identity, bias=ob_sb[:])
         ps_top = psum_other.tile([D, B], F32, name="ps_top", tag="other")
         nc.tensor.matmul(ps_top[:], wc1_sb[:], z[:], start=True, stop=True)
         top = work.tile([D, B], F32, name="top")

@@ -38,6 +38,10 @@ def tile_bilinearmlpembedpheno_b_kernel(
         tc.psum_pool(name="psum_other", bufs=1) as psum_other,
         tc.psum_pool(name="psum_z", bufs=1) as psum_z,
     ):
+        wp1_sb = held.tile([D, HC, 2], F32, name="wp1_sb")
+        nc.sync.dma_start(wp1_sb[:], wp1.rearrange("(p c) j -> p c j", c=HC))
+        ph_bc = held.tile([D, 2 * B], F32, name="ph_bc")
+        nc.sync.dma_start(ph_bc[:], phenos.rearrange("j t -> (j t)").partition_broadcast(D))
         offsets = held.tile([D, N // 16], U16, name="offsets")
         nc.sync.dma_start(offsets[:], offs)
         w1_sb = held.tile([D, D], BF16, name="w1_sb")
@@ -50,10 +54,6 @@ def tile_bilinearmlpembedpheno_b_kernel(
         nc.sync.dma_start(b1_sb[:], b1)
         b2_sb = held.tile([D, 1], F32, name="b2_sb")
         nc.sync.dma_start(b2_sb[:], b2)
-        wp1_sb = held.tile([D, HC, 2], F32, name="wp1_sb")
-        nc.sync.dma_start(wp1_sb[:], wp1.rearrange("(p c) j -> p c j", c=HC))
-        ph_bc = held.tile([D, 2 * B], F32, name="ph_bc")
-        nc.sync.dma_start(ph_bc[:], phenos.rearrange("j t -> (j t)").partition_broadcast(D))
         wb_half = []
         for s in range(2):
             wb_s = held.tile([D, HALF, D], BF16, name=f"wb_{s}")
@@ -70,6 +70,17 @@ def tile_bilinearmlpembedpheno_b_kernel(
         ident = held.tile([D, D], F32, name="ident")
         make_identity(nc, ident[:])
 
+        q1 = held.tile([D, HC, B], BF16, name="q1")
+        args = []
+        for c in range(HC):
+            part = work.tile([D, B], F32, name="part")
+            nc.vector.tensor_scalar_mul(part[:], ph_bc[:, 0:B], wp1_sb[:, c, 0:1])
+            arg = held.tile([D, B], F32, name=f"arg_{c}")
+            nc.vector.scalar_tensor_tensor(
+                arg[:], ph_bc[:, B : 2 * B], wp1_sb[:, c, 1:2], part[:], op0=ALU.mult, op1=ALU.add
+            )
+            args.append(arg)
+
         ps_a1 = []
         for half in range(2):
             ps = psum_u.tile([D, B], F32, name=f"ps_a1_{half}", tag="ps_u")
@@ -85,16 +96,6 @@ def tile_bilinearmlpembedpheno_b_kernel(
             h_half = held.tile([D, B], BF16, name=f"h_{half}")
             nc.vector.tensor_scalar_add(h_half[:], ps_h[:], b2_sb[:])
             h.append(h_half)
-
-        q1 = held.tile([D, HC, B], BF16, name="q1")
-        for c in range(HC):
-            part = work.tile([D, B], F32, name="part")
-            nc.scalar.activation(part[:], ph_bc[:, 0:B], FN.Copy, scale=wp1_sb[:, c, 0:1])
-            arg = work.tile([D, B], F32, name="arg")
-            nc.vector.scalar_tensor_tensor(
-                arg[:], ph_bc[:, B : 2 * B], wp1_sb[:, c, 1:2], part[:], op0=ALU.mult, op1=ALU.add
-            )
-            nc.scalar.activation(q1[:, c, :], arg[:], FN.Gelu)
 
         def pheno_block(y):
             ps_q2 = psum_other.tile([D, B], F32, name="ps_q2", tag="other")
@@ -158,12 +159,16 @@ def tile_bilinearmlpembedpheno_b_kernel(
                 unit_gpsimd(*divmod(step, TB))
             if step >= LEAD:
                 unit_vector(*divmod(step - LEAD, TB))
+            if 2 <= step < 2 + HC:
+                nc.scalar.activation(q1[:, step - 2, :], args[step - 2][:], FN.Gelu)
+            if step >= units + LEAD - TB:
+                tb = step - (units + LEAD - TB)
+                nc.vector.tensor_reduce(zt[tb][:, 0:IG], acc[tb][:], axis=AX.X, op=ALU.add)
             if step >= LEAD and step % HC == HC - 1:
                 pheno_block(step // HC - 1)
 
         ps_z = psum_z.tile([D, B], F32, name="ps_z")
         for tb in range(TB):
-            nc.vector.tensor_reduce(zt[tb][:, 0:IG], acc[tb][:], axis=AX.X, op=ALU.add)
             nc.tensor.transpose(ps_z[:, tb * D : (tb + 1) * D], zt[tb][:], ident[:])
         z = held.tile([D, B], BF16, name="z")
         nc.scalar.activation(z[:], ps_z[:], FN.Identity, bias=ob_sb[:])

@@ -6,7 +6,6 @@ BF16 = mybir.dt.bfloat16
 U16 = mybir.dt.uint16
 FN = mybir.ActivationFunctionType
 ALU = mybir.AluOpType
-AX = mybir.AxisListType
 
 D = 128
 S = 4096
@@ -33,10 +32,9 @@ def tile_bilinearmlpembedpheno_b_kernel(
         tc.tile_pool(name="held", bufs=1) as held,
         tc.tile_pool(name="work", bufs=4) as work,
         tc.tile_pool(name="queue", bufs=10) as queue,
-        tc.psum_pool(name="psum_u", bufs=3) as psum_u,
+        tc.psum_pool(name="psum_u", bufs=4) as psum_u,
         tc.psum_pool(name="psum_v", bufs=3) as psum_v,
         tc.psum_pool(name="psum_other", bufs=1) as psum_other,
-        tc.psum_pool(name="psum_z", bufs=1) as psum_z,
     ):
         wp1_sb = held.tile([D, HC, 2], F32, name="wp1_sb")
         nc.sync.dma_start(wp1_sb[:], wp1.rearrange("(p c) j -> p c j", c=HC))
@@ -94,7 +92,7 @@ def tile_bilinearmlpembedpheno_b_kernel(
             ps_h = psum_v.tile([D, B], F32, name="ps_h", tag="ps_v")
             nc.tensor.matmul(ps_h[:], w2_sb[:], a1[:], start=True, stop=True)
             h_half = held.tile([D, B], BF16, name=f"h_{half}")
-            nc.vector.tensor_scalar_add(h_half[:], ps_h[:], b2_sb[:])
+            nc.scalar.activation(h_half[:], ps_h[:], FN.Identity, bias=b2_sb[:])
             h.append(h_half)
 
         def pheno_block(y):
@@ -153,6 +151,17 @@ def tile_bilinearmlpembedpheno_b_kernel(
                     accum_out=zt[tb][:, i0 + r : i0 + r + 1],
                 )
 
+        def fold(tb):
+            part, width = acc[tb], AG
+            while width > 2:
+                width //= 2
+                folded = work.tile([D, IG, width], F32, name=f"folded_{width}")
+                nc.gpsimd.tensor_tensor(
+                    folded[:], part[:, :, 0:width], part[:, :, width : 2 * width], ALU.add
+                )
+                part = folded
+            nc.gpsimd.tensor_tensor(zt[tb][:, 0:IG], part[:, :, 0], part[:, :, 1], ALU.add)
+
         units = HALF
         for step in range(units + LEAD):
             if step < units:
@@ -163,17 +172,20 @@ def tile_bilinearmlpembedpheno_b_kernel(
                 nc.scalar.activation(q1[:, step - 2, :], args[step - 2][:], FN.Gelu)
             if step >= units + LEAD - TB:
                 tb = step - (units + LEAD - TB)
-                nc.vector.tensor_reduce(zt[tb][:, 0:IG], acc[tb][:], axis=AX.X, op=ALU.add)
+                fold(tb)
             if step >= LEAD and step % HC == HC - 1:
                 pheno_block(step // HC - 1)
 
-        ps_z = psum_z.tile([D, B], F32, name="ps_z")
-        for tb in range(TB):
-            nc.tensor.transpose(ps_z[:, tb * D : (tb + 1) * D], zt[tb][:], ident[:])
-        z = held.tile([D, B], BF16, name="z")
-        nc.scalar.activation(z[:], ps_z[:], FN.Identity, bias=ob_sb[:])
-        ps_top = psum_other.tile([D, B], F32, name="ps_top", tag="other")
-        nc.tensor.matmul(ps_top[:], wc1_sb[:], z[:], start=True, stop=True)
-        top = work.tile([D, B], F32, name="top")
-        nc.scalar.activation(top[:], ps_top[:], FN.Relu, bias=bc1_sb[:])
-        nc.sync.dma_start(out[0:D, :], top[:])
+        for half in range(2):
+            ps_z = psum_u.tile([D, B // 2], F32, name="ps_z", tag="ps_u")
+            for k in range(TB // 2):
+                nc.tensor.transpose(
+                    ps_z[:, k * D : (k + 1) * D], zt[half * TB // 2 + k][:], ident[:]
+                )
+            z = work.tile([D, B // 2], BF16, name="z")
+            nc.scalar.activation(z[:], ps_z[:], FN.Identity, bias=ob_sb[:])
+            ps_top = psum_v.tile([D, B // 2], F32, name="ps_top", tag="ps_v")
+            nc.tensor.matmul(ps_top[:], wc1_sb[:], z[:], start=True, stop=True)
+            top = work.tile([D, B // 2], F32, name="top")
+            nc.scalar.activation(top[:], ps_top[:], FN.Relu, bias=bc1_sb[:])
+            nc.sync.dma_start(out[0:D, half * B // 2 : (half + 1) * B // 2], top[:])

@@ -19,6 +19,8 @@ HALF = D // 2
 IG = HALF
 AG = B // IG
 IQ = B // D
+SHARE = 8
+LAG = 3
 LEAD = 8
 
 FLOPS = 2 * (2 * D * D * N + 2 * D * D * D * B + D * D * B + 2 * H * B + H * H * B)
@@ -128,7 +130,16 @@ def tile_bilinearmlpembedpheno_b_kernel(
                 nc.vector.tensor_tensor(prod[:], ps_u[:], v_sb[:], ALU.mult)
                 nc.gpsimd.tensor_tensor(acc[tb][:], acc[tb][:], prod[:], ALU.add)
 
-        def unit_vector(q, tb):
+        waiting = []
+
+        def sums_on_scalar(products, tb, i0):
+            for r in range(IQ):
+                same = work.tile([D, D], F32, name="same")
+                nc.scalar.activation(
+                    same[:], products[:, r, :], FN.Copy, accum_out=zt[tb][:, i0 + r : i0 + r + 1]
+                )
+
+        def unit_vector(q, tb, step):
             h_u = h[0][:, tb * D : (tb + 1) * D]
             h_v = h[1][:, tb * D : (tb + 1) * D]
             i0 = IG + q * IQ
@@ -144,6 +155,11 @@ def tile_bilinearmlpembedpheno_b_kernel(
             )
             v_sb = work.tile([D, IQ, D], F32, name="v_sb2", tag="v_sb")
             nc.scalar.activation(v_sb[:], ps_v[:].rearrange("p a i -> p i a"), FN.Copy)
+            if step % SHARE == SHARE // 2:
+                whole = work.tile([D, IQ, D], F32, name="whole")
+                nc.vector.tensor_tensor(whole[:], ps_u[:], v_sb[:], ALU.mult)
+                waiting.append((step, whole, tb, i0))
+                return
             for r in range(IQ):
                 prod = work.tile([D, D], F32, name="prod_one")
                 nc.vector.scalar_tensor_tensor(
@@ -167,7 +183,9 @@ def tile_bilinearmlpembedpheno_b_kernel(
             if step < units:
                 unit_gpsimd(*divmod(step, TB))
             if step >= LEAD:
-                unit_vector(*divmod(step - LEAD, TB))
+                unit_vector(*divmod(step - LEAD, TB), step)
+            if waiting and waiting[0][0] == step - LAG:
+                sums_on_scalar(*waiting.pop()[1:])
             if 2 <= step < 2 + HC:
                 nc.scalar.activation(q1[:, step - 2, :], args[step - 2][:], FN.Gelu)
             if step >= units + LEAD - TB:

@@ -181,16 +181,19 @@ def tile_bilinearmlpembedpheno_b_kernel(
         units = HALF
         for step in range(units + LEAD):
             if step < units:
-                unit_gpsimd(*divmod(step, TB))
+                half, rest = divmod(step, units // 2)
+                two, rest = divmod(rest, units // 2 // (TB // 2))
+                g, tb = divmod(rest, 2)
+                g, tb = g + half * HALF // AG, tb + 2 * two
+                unit_gpsimd(g, tb)
+                if g == D // AG - 1:
+                    fold(tb)
             if step >= LEAD:
                 unit_vector(*divmod(step - LEAD, TB), step)
             if waiting and waiting[0][0] == step - LAG:
                 sums_on_scalar(*waiting.pop()[1:])
             if 2 <= step < 2 + HC:
                 nc.scalar.activation(q1[:, step - 2, :], args[step - 2][:], FN.Gelu)
-            if step >= units + LEAD - TB:
-                tb = step - (units + LEAD - TB)
-                fold(tb)
             if step >= LEAD and step % HC == HC - 1:
                 pheno_block(step // HC - 1)
 

@@ -16,11 +16,13 @@ HC = H // D
 PIECE = B // 16
 TB = B // D
 HALF = D // 2
+QUARTER = D // 4
 IG = HALF
 AG = B // IG
 IQ = B // D
-SHARE = 8
+SHARE = 4
 LAG = 3
+EARLY = 8
 LEAD = 8
 
 FLOPS = 2 * (2 * D * D * N + 2 * D * D * D * B + D * D * B + 2 * H * B + H * H * B)
@@ -54,11 +56,9 @@ def tile_bilinearmlpembedpheno_b_kernel(
         nc.sync.dma_start(b1_sb[:], b1)
         b2_sb = held.tile([D, 1], F32, name="b2_sb")
         nc.sync.dma_start(b2_sb[:], b2)
-        wb_half = []
-        for s in range(2):
-            wb_s = held.tile([D, HALF, D], BF16, name=f"wb_{s}")
-            nc.sync.dma_start(wb_s[:], wb[:, s * HALF : (s + 1) * HALF, :])
-            wb_half.append(wb_s)
+        wb_sb = held.tile([D, D, D], BF16, name="wb_sb")
+        for first, end in ((0, QUARTER), (QUARTER, HALF), (HALF, D)):
+            nc.sync.dma_start(wb_sb[:, first:end, :], wb[:, first:end, :])
         wp2_sb = held.tile([D, HC, H], BF16, name="wp2_sb")
         nc.sync.dma_start(wp2_sb[:], wp2.rearrange("(p c) y -> p c y", c=HC))
         wc1_sb = held.tile([D, D], BF16, name="wc1_sb")
@@ -111,24 +111,23 @@ def tile_bilinearmlpembedpheno_b_kernel(
         zt = [held.tile([D, D], F32, name=f"zt_{tb}") for tb in range(TB)]
         acc = [held.tile([D, IG, AG], F32, name=f"acc_{tb}") for tb in range(TB)]
 
-        def unit_gpsimd(g, tb):
+        def unit_gpsimd(g, tb, i0=0, i1=IG):
             h_u = h[0][:, tb * D : (tb + 1) * D]
             h_v = h[1][:, tb * D : (tb + 1) * D]
-            s, a0 = divmod(g * AG, HALF)
-            ps_v = psum_v.tile([D, AG, IG], F32, name="ps_v", tag="ps_v")
-            nc.tensor.matmul(ps_v[:], h_v, wb_half[s][:, a0 : a0 + AG, 0:IG], start=True, stop=True)
-            ps_u = psum_u.tile([D, IG, AG], F32, name="ps_u", tag="ps_u")
-            nc.tensor.matmul(
-                ps_u[:], h_u, wb_half[0][:, 0:IG, g * AG : (g + 1) * AG], start=True, stop=True
-            )
-            v_sb = work.tile([D, IG, AG], F32, name="v_sb")
+            group = slice(g * AG, (g + 1) * AG)
+            ps_v = psum_v.tile([D, AG, i1 - i0], F32, name="ps_v", tag="ps_v")
+            nc.tensor.matmul(ps_v[:], h_v, wb_sb[:, group, i0:i1], start=True, stop=True)
+            ps_u = psum_u.tile([D, i1 - i0, AG], F32, name="ps_u", tag="ps_u")
+            nc.tensor.matmul(ps_u[:], h_u, wb_sb[:, i0:i1, group], start=True, stop=True)
+            v_sb = work.tile([D, i1 - i0, AG], F32, name="v_sb", tag="v_sb")
             nc.scalar.activation(v_sb[:], ps_v[:].rearrange("p a i -> p i a"), FN.Copy)
+            total = acc[tb][:, i0:i1, :]
             if g == 0:
-                nc.vector.tensor_tensor(acc[tb][:], ps_u[:], v_sb[:], ALU.mult)
+                nc.vector.tensor_tensor(total, ps_u[:], v_sb[:], ALU.mult)
             else:
-                prod = queue.tile([D, IG, AG], F32, name="prod")
+                prod = queue.tile([D, i1 - i0, AG], F32, name="prod", tag="prod")
                 nc.vector.tensor_tensor(prod[:], ps_u[:], v_sb[:], ALU.mult)
-                nc.gpsimd.tensor_tensor(acc[tb][:], acc[tb][:], prod[:], ALU.add)
+                nc.gpsimd.tensor_tensor(total, total, prod[:], ALU.add)
 
         waiting = []
 
@@ -144,18 +143,12 @@ def tile_bilinearmlpembedpheno_b_kernel(
             h_v = h[1][:, tb * D : (tb + 1) * D]
             i0 = IG + q * IQ
             ps_v = psum_v.tile([D, D, IQ], F32, name="ps_v2", tag="ps_v")
-            for s in range(2):
-                nc.tensor.matmul(
-                    ps_v[:, s * HALF : (s + 1) * HALF, :], h_v, wb_half[s][:, :, i0 : i0 + IQ],
-                    start=True, stop=True,
-                )
+            nc.tensor.matmul(ps_v[:], h_v, wb_sb[:, :, i0 : i0 + IQ], start=True, stop=True)
             ps_u = psum_u.tile([D, IQ, D], F32, name="ps_u2", tag="ps_u")
-            nc.tensor.matmul(
-                ps_u[:], h_u, wb_half[1][:, i0 - HALF : i0 - HALF + IQ, :], start=True, stop=True
-            )
+            nc.tensor.matmul(ps_u[:], h_u, wb_sb[:, i0 : i0 + IQ, :], start=True, stop=True)
             v_sb = work.tile([D, IQ, D], F32, name="v_sb2", tag="v_sb")
             nc.scalar.activation(v_sb[:], ps_v[:].rearrange("p a i -> p i a"), FN.Copy)
-            if step % SHARE == SHARE // 2:
+            if step % SHARE == 0:
                 whole = work.tile([D, IQ, D], F32, name="whole")
                 nc.vector.tensor_tensor(whole[:], ps_u[:], v_sb[:], ALU.mult)
                 waiting.append((step, whole, tb, i0))
@@ -178,16 +171,24 @@ def tile_bilinearmlpembedpheno_b_kernel(
                 part = folded
             nc.gpsimd.tensor_tensor(zt[tb][:, 0:IG], part[:, :, 0], part[:, :, 1], ALU.add)
 
+        def sums_of_gpsimd(step):
+            half, rest = divmod(step, units // 2)
+            two, rest = divmod(rest, units // 4)
+            g, tb = divmod(rest, 2)
+            g, tb = g + half * HALF // AG, tb + 2 * two
+            if step < EARLY:
+                i0 = 2 * step // EARLY * QUARTER
+                for k in range(2 * step, 2 * step + 2):
+                    unit_gpsimd(k % EARLY // 2, k % 2, i0, i0 + QUARTER)
+            else:
+                unit_gpsimd(g, tb)
+            if g == D // AG - 1:
+                fold(tb)
+
         units = HALF
         for step in range(units + LEAD):
             if step < units:
-                half, rest = divmod(step, units // 2)
-                two, rest = divmod(rest, units // 2 // (TB // 2))
-                g, tb = divmod(rest, 2)
-                g, tb = g + half * HALF // AG, tb + 2 * two
-                unit_gpsimd(g, tb)
-                if g == D // AG - 1:
-                    fold(tb)
+                sums_of_gpsimd(step)
             if step >= LEAD:
                 unit_vector(*divmod(step - LEAD, TB), step)
             if waiting and waiting[0][0] == step - LAG:

@@ -13,7 +13,7 @@ B = 512
 N = 2 * B
 H = 1024
 HC = H // D
-PIECE = B // 16
+PIECE = B // 2 // 16
 TB = B // D
 HALF = D // 2
 QUARTER = D // 4
@@ -71,31 +71,38 @@ def tile_bilinearmlpembedpheno_b_kernel(
         make_identity(nc, ident[:])
 
         q1 = held.tile([D, HC, B], BF16, name="q1")
-        args = []
-        for c in range(HC):
-            part = work.tile([D, B], F32, name="part")
-            nc.vector.tensor_scalar_mul(part[:], ph_bc[:, 0:B], wp1_sb[:, c, 0:1])
-            arg = held.tile([D, B], F32, name=f"arg_{c}")
-            nc.vector.scalar_tensor_tensor(
-                arg[:], ph_bc[:, B : 2 * B], wp1_sb[:, c, 1:2], part[:], op0=ALU.mult, op1=ALU.add
-            )
-            args.append(arg)
+        parts, args = [], []
+        for step in range(HC + 1):
+            if step < HC:
+                part = work.tile([D, B], F32, name="part")
+                nc.vector.tensor_scalar_mul(part[:], ph_bc[:, 0:B], wp1_sb[:, step, 0:1])
+                parts.append(part)
+            if step > 0:
+                c = step - 1
+                arg = held.tile([D, B], F32, name=f"arg_{c}")
+                nc.vector.scalar_tensor_tensor(
+                    arg[:], ph_bc[:, B : 2 * B], wp1_sb[:, c, 1:2], parts[c][:],
+                    op0=ALU.mult, op1=ALU.add,
+                )
+                args.append(arg)
 
+        pieces = [(gene, part) for part in range(2) for gene in range(2)]
         ps_a1 = []
-        for half in range(2):
-            ps = psum_u.tile([D, B], F32, name=f"ps_a1_{half}", tag="ps_u")
-            looked_up = table_sb[:].indirect(offsets[:, half * PIECE : (half + 1) * PIECE])
+        for gene, part in pieces:
+            ps = psum_u.tile([D, B // 2], F32, name=f"ps_a1_{gene}_{part}", tag="ps_u")
+            first = (2 * gene + part) * PIECE
+            looked_up = table_sb[:].indirect(offsets[:, first : first + PIECE])
             nc.tensor.matmul(ps[:], w1_sb[:], looked_up, start=True, stop=True)
             ps_a1.append(ps)
-        h = []
-        for half in range(2):
-            a1 = work.tile([D, B], BF16, name="a1")
-            nc.scalar.activation(a1[:], ps_a1[half][:], FN.Relu, bias=b1_sb[:])
-            ps_h = psum_v.tile([D, B], F32, name="ps_h", tag="ps_v")
+        h = [held.tile([D, B], BF16, name=f"h_{gene}") for gene in range(2)]
+        for k, (gene, part) in enumerate(pieces):
+            a1 = work.tile([D, B // 2], BF16, name="a1")
+            nc.scalar.activation(a1[:], ps_a1[k][:], FN.Relu, bias=b1_sb[:])
+            ps_h = psum_v.tile([D, B // 2], F32, name="ps_h", tag="ps_v")
             nc.tensor.matmul(ps_h[:], w2_sb[:], a1[:], start=True, stop=True)
-            h_half = held.tile([D, B], BF16, name=f"h_{half}")
-            nc.scalar.activation(h_half[:], ps_h[:], FN.Identity, bias=b2_sb[:])
-            h.append(h_half)
+            nc.scalar.activation(
+                h[gene][:, part * B // 2 : (part + 1) * B // 2], ps_h[:], FN.Identity, bias=b2_sb[:]
+            )
 
         def pheno_block(y):
             ps_q2 = psum_other.tile([D, B], F32, name="ps_q2", tag="other")
@@ -198,16 +205,13 @@ def tile_bilinearmlpembedpheno_b_kernel(
             if step >= LEAD and step % HC == HC - 1:
                 pheno_block(step // HC - 1)
 
-        for half in range(2):
-            ps_z = psum_u.tile([D, B // 2], F32, name="ps_z", tag="ps_u")
-            for k in range(TB // 2):
-                nc.tensor.transpose(
-                    ps_z[:, k * D : (k + 1) * D], zt[half * TB // 2 + k][:], ident[:]
-                )
-            z = work.tile([D, B // 2], BF16, name="z")
+        for tb in range(TB):
+            ps_z = psum_u.tile([D, D], F32, name="ps_z", tag="ps_u")
+            nc.tensor.transpose(ps_z[:], zt[tb][:], ident[:])
+            z = work.tile([D, D], BF16, name="z")
             nc.scalar.activation(z[:], ps_z[:], FN.Identity, bias=ob_sb[:])
-            ps_top = psum_v.tile([D, B // 2], F32, name="ps_top", tag="ps_v")
+            ps_top = psum_v.tile([D, D], F32, name="ps_top", tag="ps_v")
             nc.tensor.matmul(ps_top[:], wc1_sb[:], z[:], start=True, stop=True)
-            top = work.tile([D, B // 2], F32, name="top")
+            top = work.tile([D, D], F32, name="top")
             nc.scalar.activation(top[:], ps_top[:], FN.Relu, bias=bc1_sb[:])
-            nc.sync.dma_start(out[0:D, half * B // 2 : (half + 1) * B // 2], top[:])
+            nc.sync.dma_start(out[0:D, tb * D : (tb + 1) * D], top[:])

import concourse.mybir as mybir
from concourse.masks import make_identity

F32 = mybir.dt.float32
BF16 = mybir.dt.bfloat16
U16 = mybir.dt.uint16
FN = mybir.ActivationFunctionType
ALU = mybir.AluOpType

D = 128
S = 4096
B = 512
N = 2 * B
H = 1024
HC = H // D
PIECE = B // 2 // 16
TB = B // D
HALF = D // 2
QUARTER = D // 4
IG = HALF
AG = B // IG
IQ = B // D
SHARE = 4
LAG = 3
EARLY = 8
LEAD = 8

FLOPS = 2 * (2 * D * D * N + 2 * D * D * D * B + D * D * B + 2 * H * B + H * H * B)


def tile_bilinearmlpembedpheno_b_kernel(
    tc, table, w1, b1, w2, b2, wb, ob, wc1, bc1, phenos, wp1, wp2, offs, out
):
    nc = tc.nc
    with (
        tc.tile_pool(name="held", bufs=1) as held,
        tc.tile_pool(name="work", bufs=4) as work,
        tc.tile_pool(name="queue", bufs=10) as queue,
        tc.psum_pool(name="psum_u", bufs=4) as psum_u,
        tc.psum_pool(name="psum_v", bufs=3) as psum_v,
        tc.psum_pool(name="psum_other", bufs=1) as psum_other,
    ):
        wp1_sb = held.tile([D, HC, 2], F32, name="wp1_sb")
        nc.sync.dma_start(wp1_sb[:], wp1.rearrange("(p c) j -> p c j", c=HC))
        ph_bc = held.tile([D, 2 * B], F32, name="ph_bc")
        nc.sync.dma_start(ph_bc[:], phenos.rearrange("j t -> (j t)").partition_broadcast(D))
        offsets = held.tile([D, N // 16], U16, name="offsets")
        nc.sync.dma_start(offsets[:], offs)
        w1_sb = held.tile([D, D], BF16, name="w1_sb")
        nc.sync.dma_start(w1_sb[:], w1)
        table_sb = held.tile([D, S], BF16, name="table_sb")
        nc.sync.dma_start(table_sb[:], table)
        w2_sb = held.tile([D, D], BF16, name="w2_sb")
        nc.sync.dma_start(w2_sb[:], w2)
        b1_sb = held.tile([D, 1], F32, name="b1_sb")
        nc.sync.dma_start(b1_sb[:], b1)
        b2_sb = held.tile([D, 1], F32, name="b2_sb")
        nc.sync.dma_start(b2_sb[:], b2)
        wb_sb = held.tile([D, D, D], BF16, name="wb_sb")
        for first, end in ((0, QUARTER), (QUARTER, HALF), (HALF, D)):
            nc.sync.dma_start(wb_sb[:, first:end, :], wb[:, first:end, :])
        wp2_sb = held.tile([D, HC, H], BF16, name="wp2_sb")
        nc.sync.dma_start(wp2_sb[:], wp2.rearrange("(p c) y -> p c y", c=HC))
        wc1_sb = held.tile([D, D], BF16, name="wc1_sb")
        nc.sync.dma_start(wc1_sb[:], wc1)
        ob_sb = held.tile([D, 1], F32, name="ob_sb")
        nc.sync.dma_start(ob_sb[:], ob)
        bc1_sb = held.tile([D, 1], F32, name="bc1_sb")
        nc.sync.dma_start(bc1_sb[:], bc1)
        ident = held.tile([D, D], F32, name="ident")
        make_identity(nc, ident[:])

        q1 = held.tile([D, HC, B], BF16, name="q1")
        parts, args = [], []
        for step in range(HC + 1):
            if step < HC:
                part = work.tile([D, B], F32, name="part")
                nc.vector.tensor_scalar_mul(part[:], ph_bc[:, 0:B], wp1_sb[:, step, 0:1])
                parts.append(part)
            if step > 0:
                c = step - 1
                arg = held.tile([D, B], F32, name=f"arg_{c}")
                nc.vector.scalar_tensor_tensor(
                    arg[:], ph_bc[:, B : 2 * B], wp1_sb[:, c, 1:2], parts[c][:],
                    op0=ALU.mult, op1=ALU.add,
                )
                args.append(arg)

        pieces = [(gene, part) for part in range(2) for gene in range(2)]
        ps_a1 = []
        for gene, part in pieces:
            ps = psum_u.tile([D, B // 2], F32, name=f"ps_a1_{gene}_{part}", tag="ps_u")
            first = (2 * gene + part) * PIECE
            looked_up = table_sb[:].indirect(offsets[:, first : first + PIECE])
            nc.tensor.matmul(ps[:], w1_sb[:], looked_up, start=True, stop=True)
            ps_a1.append(ps)
        h = [held.tile([D, B], BF16, name=f"h_{gene}") for gene in range(2)]
        for k, (gene, part) in enumerate(pieces):
            a1 = work.tile([D, B // 2], BF16, name="a1")
            nc.scalar.activation(a1[:], ps_a1[k][:], FN.Relu, bias=b1_sb[:])
            ps_h = psum_v.tile([D, B // 2], F32, name="ps_h", tag="ps_v")
            nc.tensor.matmul(ps_h[:], w2_sb[:], a1[:], start=True, stop=True)
            nc.scalar.activation(
                h[gene][:, part * B // 2 : (part + 1) * B // 2], ps_h[:], FN.Identity, bias=b2_sb[:]
            )

        def pheno_block(y):
            ps_q2 = psum_other.tile([D, B], F32, name="ps_q2", tag="other")
            for c in range(HC):
                nc.tensor.matmul(
                    ps_q2[:], wp2_sb[:, c, y * D : (y + 1) * D], q1[:, c, :],
                    start=(c == 0), stop=(c == HC - 1),
                )
            q2 = work.tile([D, B], F32, name="q2")
            nc.scalar.activation(q2[:], ps_q2[:], FN.Gelu)
            nc.sync.dma_start(out[(y + 1) * D : (y + 2) * D, :], q2[:])

        zt = [held.tile([D, D], F32, name=f"zt_{tb}") for tb in range(TB)]
        acc = [held.tile([D, IG, AG], F32, name=f"acc_{tb}") for tb in range(TB)]

        def unit_gpsimd(g, tb, i0=0, i1=IG):
            h_u = h[0][:, tb * D : (tb + 1) * D]
            h_v = h[1][:, tb * D : (tb + 1) * D]
            group = slice(g * AG, (g + 1) * AG)
            ps_v = psum_v.tile([D, AG, i1 - i0], F32, name="ps_v", tag="ps_v")
            nc.tensor.matmul(ps_v[:], h_v, wb_sb[:, group, i0:i1], start=True, stop=True)
            ps_u = psum_u.tile([D, i1 - i0, AG], F32, name="ps_u", tag="ps_u")
            nc.tensor.matmul(ps_u[:], h_u, wb_sb[:, i0:i1, group], start=True, stop=True)
            v_sb = work.tile([D, i1 - i0, AG], F32, name="v_sb", tag="v_sb")
            nc.scalar.activation(v_sb[:], ps_v[:].rearrange("p a i -> p i a"), FN.Copy)
            total = acc[tb][:, i0:i1, :]
            if g == 0:
                nc.vector.tensor_tensor(total, ps_u[:], v_sb[:], ALU.mult)
            else:
                prod = queue.tile([D, i1 - i0, AG], F32, name="prod", tag="prod")
                nc.vector.tensor_tensor(prod[:], ps_u[:], v_sb[:], ALU.mult)
                nc.gpsimd.tensor_tensor(total, total, prod[:], ALU.add)

        waiting = []

        def sums_on_scalar(products, tb, i0):
            for r in range(IQ):
                same = work.tile([D, D], F32, name="same")
                nc.scalar.activation(
                    same[:], products[:, r, :], FN.Copy, accum_out=zt[tb][:, i0 + r : i0 + r + 1]
                )

        def unit_vector(q, tb, step):
            h_u = h[0][:, tb * D : (tb + 1) * D]
            h_v = h[1][:, tb * D : (tb + 1) * D]
            i0 = IG + q * IQ
            ps_v = psum_v.tile([D, D, IQ], F32, name="ps_v2", tag="ps_v")
            nc.tensor.matmul(ps_v[:], h_v, wb_sb[:, :, i0 : i0 + IQ], start=True, stop=True)
            ps_u = psum_u.tile([D, IQ, D], F32, name="ps_u2", tag="ps_u")
            nc.tensor.matmul(ps_u[:], h_u, wb_sb[:, i0 : i0 + IQ, :], start=True, stop=True)
            v_sb = work.tile([D, IQ, D], F32, name="v_sb2", tag="v_sb")
            nc.scalar.activation(v_sb[:], ps_v[:].rearrange("p a i -> p i a"), FN.Copy)
            if step % SHARE == 0:
                whole = work.tile([D, IQ, D], F32, name="whole")
                nc.vector.tensor_tensor(whole[:], ps_u[:], v_sb[:], ALU.mult)
                waiting.append((step, whole, tb, i0))
                return
            for r in range(IQ):
                prod = work.tile([D, D], F32, name="prod_one")
                nc.vector.scalar_tensor_tensor(
                    prod[:], ps_u[:, r, :], 1.0, v_sb[:, r, :], op0=ALU.mult, op1=ALU.mult,
                    accum_out=zt[tb][:, i0 + r : i0 + r + 1],
                )

        def fold(tb):
            part, width = acc[tb], AG
            while width > 2:
                width //= 2
                folded = work.tile([D, IG, width], F32, name=f"folded_{width}")
                nc.gpsimd.tensor_tensor(
                    folded[:], part[:, :, 0:width], part[:, :, width : 2 * width], ALU.add
                )
                part = folded
            nc.gpsimd.tensor_tensor(zt[tb][:, 0:IG], part[:, :, 0], part[:, :, 1], ALU.add)

        def sums_of_gpsimd(step):
            half, rest = divmod(step, units // 2)
            two, rest = divmod(rest, units // 4)
            g, tb = divmod(rest, 2)
            g, tb = g + half * HALF // AG, tb + 2 * two
            if step < EARLY:
                i0 = 2 * step // EARLY * QUARTER
                for k in range(2 * step, 2 * step + 2):
                    unit_gpsimd(k % EARLY // 2, k % 2, i0, i0 + QUARTER)
            else:
                unit_gpsimd(g, tb)
            if g == D // AG - 1:
                fold(tb)

        units = HALF
        for step in range(units + LEAD):
            if step < units:
                sums_of_gpsimd(step)
            if step >= LEAD:
                unit_vector(*divmod(step - LEAD, TB), step)
            if waiting and waiting[0][0] == step - LAG:
                sums_on_scalar(*waiting.pop()[1:])
            if 2 <= step < 2 + HC:
                nc.scalar.activation(q1[:, step - 2, :], args[step - 2][:], FN.Gelu)
            if step >= LEAD and step % HC == HC - 1:
                pheno_block(step // HC - 1)

        for tb in range(TB):
            ps_z = psum_u.tile([D, D], F32, name="ps_z", tag="ps_u")
            nc.tensor.transpose(ps_z[:], zt[tb][:], ident[:])
            z = work.tile([D, D], BF16, name="z")
            nc.scalar.activation(z[:], ps_z[:], FN.Identity, bias=ob_sb[:])
            ps_top = psum_v.tile([D, D], F32, name="ps_top", tag="ps_v")
            nc.tensor.matmul(ps_top[:], wc1_sb[:], z[:], start=True, stop=True)
            top = work.tile([D, D], F32, name="top")
            nc.scalar.activation(top[:], ps_top[:], FN.Relu, bias=bc1_sb[:])
            nc.sync.dma_start(out[0:D, tb * D : (tb + 1) * D], top[:])
